import numpy as np
import ml_dtypes


def mxq(x, axis, fmt="e4m3"):
    dtype, down = {"e4m3": (ml_dtypes.float8_e4m3fn, 7), "e5m2": (ml_dtypes.float8_e5m2, 14)}[fmt]
    v = np.moveaxis(np.asarray(x, np.float32).astype(ml_dtypes.bfloat16).astype(np.float64), axis, -1)
    blocks = v.reshape(v.shape[:-1] + (-1, 32))
    amax = np.abs(blocks).max(-1, keepdims=True)
    byte = np.maximum(np.where(amax > 0, np.frexp(amax)[1] - 1 + 127, 0) - down, 1)
    scale = np.exp2(byte - 127.0)
    codes = (blocks / scale).astype(np.float32).astype(dtype).astype(np.float64)
    return np.moveaxis((codes * scale).reshape(v.shape), -1, axis)


WIDE = False


def mx_kscale(k):
    if not WIDE:
        return np.ones(k)
    levels = np.array([10, -10, 5, -5, 0])
    a = np.random.permutation(np.resize(levels, k // 512 * 4)).reshape(k // 512, 4)
    idx = np.arange(k)
    return np.exp2(a[idx // 512, idx % 128 // 32])


BF16 = ml_dtypes.bfloat16


def bf(x):
    return np.asarray(x, np.float32).astype(BF16)


def f64(x):
    return np.asarray(x).astype(np.float64)


P, N, Z, H1, H2, C = 2, 4096, 16, 1024, 512, 256
EPS = 1e-5


def batch_norm(h, gamma, beta):
    mu = h.mean(axis=1, keepdims=True)
    var = h.var(axis=1, keepdims=True)
    return (h - mu) * (1.0 / np.sqrt(var + EPS)) * gamma[:, None, :] + beta[:, None, :]


def setup_inputs():
    r = np.random.standard_normal
    t = mx_kscale(H1)
    sd = np.where(np.random.random((P, 1, H1)) < 0.25, np.sqrt(EPS), 1.0)
    return {"h6_pre": bf((r((P, N, H1)) + 0.5 * r((P, 1, H1))) * sd),
            "g6": bf((1.0 + 0.1 * r((P, H1))) * t),
            "be6": bf(0.3 * r((P, H1)) * t),
            "W7": bf(r((P, H2, H1)) / np.sqrt(H1) / t),
            "b7": bf(0.3 * r((P, H2)))}


def reference(h6_pre, g6, be6, W7, b7):
    a = np.maximum(batch_norm(f64(h6_pre), f64(g6), f64(be6)), 0.0)
    y = mxq(a, 2, "e4m3") @ mxq(f64(W7), 2, "e4m3").transpose(0, 2, 1)
    return y + f64(b7)[:, None, :]

@@ -1,0 +1,273 @@
+from contextlib import ExitStack
+
+import concourse.bass as bass
+import concourse.mybir as mybir
+import concourse.tile as tile
+from concourse.masks import make_identity
+
+F32 = mybir.dt.float32
+BF16 = mybir.dt.bfloat16
+U32 = mybir.dt.uint32
+U8 = mybir.dt.uint8
+FP8X4 = mybir.dt.float8_e4m3fn_x4
+ALU = mybir.AluOpType
+ACT = mybir.ActivationFunctionType
+AX = mybir.AxisListType
+
+P = 128
+BLOCKS = 2
+ROWS = 4096
+K_IN = 1024
+J_OUT = 512
+PACK = 4
+K_PASS = P * PACK
+TILES = 8
+GROUP_ROWS = TILES * P
+GROUPS = ROWS // GROUP_ROWS
+UNITS = 4
+NS = 16
+EPS = 1e-5
+
+FLOPS = 2 * BLOCKS * ROWS * K_IN * J_OUT
+
+S_CHUNKS = (2, 3, 4, 4)
+S_REGROUP = (0, 0, 0, 1024)
+S_NORM = (0, 0, 0, 1)
+XT_BUFS = 10
+W_LOAD_STEP = (1, 7)
+W_PREP_STEP = (5, 10)
+
+
+def tile_decoder_pa_t_kernel(tc, h6_pre, g6, be6, W7, b7, out):
+    nc = tc.nc
+    with ExitStack() as ctx:
+        const = ctx.enter_context(tc.tile_pool(name="const", bufs=1))
+        natp = ctx.enter_context(tc.tile_pool(name="natp", bufs=4))
+        xtp = ctx.enter_context(tc.tile_pool(name="xtp", bufs=XT_BUFS))
+        statp = ctx.enter_context(tc.tile_pool(name="statp", bufs=2))
+        plp = ctx.enter_context(tc.tile_pool(name="plp", bufs=2))
+        grp = ctx.enter_context(tc.tile_pool(name="grp", bufs=2))
+        acp = ctx.enter_context(tc.tile_pool(name="acp", bufs=2))
+        osbp = ctx.enter_context(tc.tile_pool(name="osbp", bufs=2))
+        wp = ctx.enter_context(tc.tile_pool(name="wp", bufs=1))
+        tps = ctx.enter_context(tc.psum_pool(name="tps", bufs=3))
+        sump = ctx.enter_context(tc.psum_pool(name="sump", bufs=2))
+        accp = ctx.enter_context(tc.psum_pool(name="accp", bufs=3))
+
+        warm = const.tile([P, 2], F32, name="warm")
+        nc.vector.memset(warm[:], 1.0)
+        nc.scalar.activation(out=warm[:, 1:2], in_=warm[:, 0:1], func=ACT.Sqrt)
+        ident = const.tile([P, P], BF16, name="ident")
+        make_identity(nc, ident[:])
+        ones = const.tile([P, P], BF16, name="ones")
+        nc.vector.memset(ones[:], 1.0)
+        rows = const.tile([P, P], BF16, name="rows")
+        nc.vector.memset(rows[:], 0.0)
+        brow = const.tile([P, BLOCKS * J_OUT], BF16, name="brow")
+        nc.vector.memset(brow[:], 0.0)
+        nc.scalar.dma_start(out=rows[0:16, :], in_=g6.rearrange("b (c q) -> (b c) q", q=P))
+        nc.scalar.dma_start(out=rows[16:32, :], in_=be6.rearrange("b (c q) -> (b c) q", q=P))
+        nc.scalar.dma_start(out=brow[0:1, :], in_=b7.rearrange("(o b) j -> o (b j)", o=1))
+        junk = const.tile([P, GROUP_ROWS], BF16, name="junk")
+        gb = const.tile([P, 32], F32, name="gb")
+        bias = const.tile([P, BLOCKS, J_OUT], F32, name="bias")
+        wc = const.tile([P, BLOCKS, 2, J_OUT], U32, name="wc", align_bytes=64)
+        ws = const.tile([P, BLOCKS, 2, J_OUT], U8, name="ws", align_bytes=64)
+        ac0 = const.tile([P, ROWS], U32, name="ac0", align_bytes=64)
+        as0 = const.tile([P, ROWS], U8, name="as0", align_bytes=64)
+
+        def small_params():
+            tp = tps.tile([P, TILES, P], BF16, name="tp")
+            nc.tensor.transpose(tp[:, 0, :], rows[:], ident[:])
+            nc.vector.tensor_copy(out=gb[:], in_=tp[:, 0, 0:32])
+            for b in range(BLOCKS):
+                acc = accp.tile([P, J_OUT], F32, name="acc")
+                nc.tensor.matmul(out=acc[:], lhsT=ones[:], rhs=brow[:, b * J_OUT:(b + 1) * J_OUT],
+                                 start=True, stop=True)
+                nc.vector.tensor_copy(out=bias[:, b, :], in_=acc[:])
+
+        def grouped_views(dst, src):
+            return (dst.rearrange("p (c i) t -> p c t i", i=4),
+                    src.rearrange("p t (c i) -> p c t i", i=4))
+
+        def w_load(b):
+            wn = natp.tile([P, 4, K_IN], BF16, name="nat")
+            nc.sync.dma_start(out=wn[:], in_=W7[b].rearrange("(a o) k -> o a k", o=P))
+            return wn
+
+        def w_prep(b, wn):
+            for g in range(2):
+                wpl = wp.tile([P, PACK, J_OUT], BF16, name="wpl")
+                for h in range(2):
+                    tp = tps.tile([P, TILES, P], BF16, name="tp")
+                    for jj in range(2):
+                        c = g * PACK + 2 * h + jj
+                        for a in range(4):
+                            nc.tensor.transpose(tp[:, jj * 4 + a, :], wn[:, a, c * P:(c + 1) * P], ident[:])
+                    nc.scalar.copy(out=wpl[:, 2 * h:2 * h + 2, :].rearrange("q j o -> q (j o)").bitcast(F32),
+                                   in_=tp[:].rearrange("q t n -> q (t n)").bitcast(F32))
+                wgr = wp.tile([P, J_OUT, PACK], BF16, name="wgr", align_bytes=64)
+                d, s = grouped_views(wgr[:], wpl[:])
+                nc.vector.tensor_copy(out=d, in_=s)
+                nc.vector.quantize_mx(out=wc[:, b, g, :].bitcast(FP8X4), scales=ws[:, b, g, :],
+                                      in_=wgr[:].rearrange("p n t -> p (n t)"))
+
+        st = {}
+
+        def load(u, r):
+            b, g = divmod(u, 2)
+            nat = natp.tile([P, TILES, K_PASS], BF16, name="nat")
+            nc.sync.dma_start(
+                out=nat[:],
+                in_=h6_pre[b, r * GROUP_ROWS:(r + 1) * GROUP_ROWS, g * K_PASS:(g + 1) * K_PASS]
+                .rearrange("(q t) k -> q t k", t=TILES))
+            return nat
+
+        def p1_open(u):
+            ns = S_CHUNKS[u]
+            d = {}
+            d["xt"] = {}
+            if ns > 0:
+                d["sq"] = statp.tile([P, PACK, GROUPS], F32, name="sq")
+                d["sums"] = sump.tile([P, GROUPS * PACK * NS], F32, name="sums")
+            if ns < PACK:
+                d["bst"] = statp.tile([P, PACK, 2 * GROUPS, 6], F32, name="bst")
+            st[u] = d
+
+        def p1(u, r, nat):
+            ns = S_CHUNKS[u]
+            d = st[u]
+            xt = xtp.tile([P, PACK, GROUP_ROWS], BF16, name="xt")
+            d["xt"][r] = xt
+            for j in range(PACK):
+                tp = tps.tile([P, TILES, P], BF16, name="tp")
+                for t in range(TILES):
+                    nc.tensor.transpose(tp[:, t, :], nat[:, t, j * P:(j + 1) * P], ident[:])
+                flat = tp[:].rearrange("q t n -> q (t n)")
+                dst = xt[:, j, :]
+                if j < ns:
+                    col = (r * PACK + j) * NS
+                    for t in range(TILES):
+                        nc.tensor.matmul(out=d["sums"][:, col:col + NS], lhsT=nat[:, t, j * P:(j + 1) * P],
+                                         rhs=ones[:, 0:NS], start=(t == 0), stop=(t == TILES - 1))
+                    nc.scalar.copy(out=dst.bitcast(F32), in_=flat.bitcast(F32))
+                    nc.scalar.activation(out=junk[:], in_=flat, func=ACT.Square, bias=d["xt"][0][:, j, 0:1],
+                                         scale=-1.0, accum_out=d["sq"][:, j, r:r + 1])
+                else:
+                    nc.vector.tensor_copy(out=dst, in_=flat)
+                    for h in range(2):
+                        nc.vector.bn_stats(out=d["bst"][:, j, 2 * r + h, :], in_=flat[:, h * 512:(h + 1) * 512])
+
+        def fin(u):
+            b, g = divmod(u, 2)
+            ns = S_CHUNKS[u]
+            d = st[u]
+            xt = d["xt"][0]
+            mv = statp.tile([P, PACK, 2], F32, name="mv")
+            if ns > 0:
+                s1 = statp.tile([P, PACK], F32, name="s1")
+                s2 = statp.tile([P, PACK], F32, name="s2")
+                df = statp.tile([P, PACK], F32, name="df")
+                nc.vector.tensor_reduce(
+                    out=s1[:, 0:ns],
+                    in_=d["sums"][:].rearrange("q (r j n) -> q j r n", r=GROUPS, j=PACK)[:, 0:ns, :, 0],
+                    axis=AX.X, op=ALU.add)
+                nc.vector.tensor_reduce(out=s2[:, 0:ns], in_=d["sq"][:, 0:ns, :], axis=AX.X, op=ALU.add)
+                nc.vector.tensor_scalar(out=mv[:, 0:ns, 0], in0=s1[:, 0:ns], scalar1=1.0 / ROWS, scalar2=None,
+                                        op0=ALU.mult)
+                nc.vector.tensor_tensor(out=df[:, 0:ns], in0=mv[:, 0:ns, 0], in1=xt[:, 0:ns, 0], op=ALU.subtract)
+                nc.vector.tensor_tensor(out=df[:, 0:ns], in0=df[:, 0:ns], in1=df[:, 0:ns], op=ALU.mult)
+                nc.vector.scalar_tensor_tensor(out=mv[:, 0:ns, 1], in0=s2[:, 0:ns], scalar=1.0 / ROWS,
+                                               in1=df[:, 0:ns], op0=ALU.mult, op1=ALU.subtract)
+            for j in range(ns, PACK):
+                nc.vector.bn_aggr(out=mv[:, j, :], in_=d["bst"][:, j, :, :].rearrange("q a s -> q (a s)"))
+            ve = statp.tile([P, PACK], F32, name="ve")
+            sd = statp.tile([P, PACK], F32, name="sd")
+            sc = statp.tile([P, PACK], F32, name="sc")
+            bi = statp.tile([P, PACK], F32, name="bi")
+            nc.vector.tensor_scalar(out=ve[:], in0=mv[:, :, 1], scalar1=0.0, scalar2=EPS, op0=ALU.max, op1=ALU.add)
+            nc.scalar.activation(out=sd[:], in_=ve[:], func=ACT.Sqrt)
+            nc.vector.reciprocal(out=ve[:], in_=sd[:])
+            c0 = b * 8 + g * PACK
+            nc.vector.tensor_tensor(out=sc[:], in0=gb[:, c0:c0 + PACK], in1=ve[:], op=ALU.mult)
+            nc.vector.tensor_tensor(out=sd[:], in0=mv[:, :, 0], in1=sc[:], op=ALU.mult)
+            nc.vector.tensor_tensor(out=bi[:], in0=gb[:, 16 + c0:16 + c0 + PACK], in1=sd[:], op=ALU.subtract)
+            d["sc"] = sc
+            d["bi"] = bi
+
+        def p2(u, r):
+            b, g = divmod(u, 2)
+            d = st[u]
+            xt = d["xt"][r]
+            pl = plp.tile([P, PACK, GROUP_ROWS], BF16, name="pl")
+            for j in range(PACK):
+                if j < PACK - S_NORM[u]:
+                    nc.vector.tensor_scalar(out=pl[:, j, :], in0=xt[:, j, :],
+                                            scalar1=d["sc"][:, j:j + 1], scalar2=d["bi"][:, j:j + 1],
+                                            op0=ALU.mult, op1=ALU.add)
+                else:
+                    nc.scalar.activation(out=pl[:, j, :], in_=xt[:, j, :], func=ACT.Relu,
+                                         bias=d["bi"][:, j:j + 1], scale=d["sc"][:, j:j + 1])
+            gr = grp.tile([P, GROUP_ROWS, PACK], BF16, name="gr", align_bytes=64)
+            cv = GROUP_ROWS - S_REGROUP[u]
+            if cv > 0:
+                dv, sv = grouped_views(gr[:, 0:cv, :], pl[:, :, 0:cv])
+                nc.vector.tensor_scalar(out=dv, in0=sv, scalar1=0.0, scalar2=None, op0=ALU.max)
+            if cv < GROUP_ROWS:
+                da, sa = grouped_views(gr[:, cv:GROUP_ROWS, :], pl[:, :, cv:GROUP_ROWS])
+                nc.scalar.activation(out=da, in_=sa, func=ACT.Relu)
+            if g == 0:
+                codes = ac0[:, r * GROUP_ROWS:(r + 1) * GROUP_ROWS]
+                scales = as0[:, r * GROUP_ROWS:(r + 1) * GROUP_ROWS]
+            else:
+                ac1 = acp.tile([P, GROUP_ROWS], U32, name="ac1", align_bytes=64)
+                as1 = acp.tile([P, GROUP_ROWS], U8, name="as1", align_bytes=64)
+                codes = ac1[:]
+                scales = as1[:]
+            nc.vector.quantize_mx(out=codes.bitcast(FP8X4), scales=scales,
+                                  in_=gr[:].rearrange("p n t -> p (n t)"))
+            if g == 0:
+                return
+            dram = out[b, r * GROUP_ROWS:(r + 1) * GROUP_ROWS, :].rearrange("(q t) j -> q t j", t=TILES)
+            for h in range(2):
+                osb = osbp.tile([P, 4, J_OUT], F32, name="osb")
+                for tt in range(4):
+                    t = 4 * h + tt
+                    c0 = r * GROUP_ROWS + t * P
+                    acc = accp.tile([P, J_OUT], F32, name="acc")
+                    nc.tensor.matmul_mx(out=acc[:], lhsT=ac0[:, c0:c0 + P].bitcast(FP8X4),
+                                        lhsT_scale=as0[:, c0:c0 + P],
+                                        rhs=wc[:, b, 0, :].bitcast(FP8X4), rhs_scale=ws[:, b, 0, :],
+                                        start=True, stop=False)
+                    nc.tensor.matmul_mx(out=acc[:], lhsT=codes[:, t * P:(t + 1) * P].bitcast(FP8X4),
+                                        lhsT_scale=scales[:, t * P:(t + 1) * P],
+                                        rhs=wc[:, b, 1, :].bitcast(FP8X4), rhs_scale=ws[:, b, 1, :],
+                                        start=False, stop=True)
+                    nc.vector.tensor_tensor(out=osb[:, tt, :], in0=acc[:], in1=bias[:, b, :], op=ALU.add)
+                nc.sync.dma_start(out=dram[:, 4 * h:4 * h + 4, :], in_=osb[:])
+
+        steps = [(u, r) for u in range(UNITS) for r in range(GROUPS)]
+        ahead = 4
+        nats = {}
+        wns = {}
+        for s in range(ahead):
+            nats[s] = load(steps[s][0], steps[s][1])
+        small_params()
+        for s in range(len(steps)):
+            u, r = steps[s]
+            if r == 0:
+                p1_open(u)
+            p1(u, r, nats[s])
+            if s + ahead < len(steps):
+                nats[s + ahead] = load(steps[s + ahead][0], steps[s + ahead][1])
+            for b in range(BLOCKS):
+                if s == W_LOAD_STEP[b]:
+                    wns[b] = w_load(b)
+                if s == W_PREP_STEP[b]:
+                    w_prep(b, wns[b])
+            if u >= 1:
+                p2(u - 1, r)
+            if r == GROUPS - 1:
+                fin(u)
+        for r in range(GROUPS):
+            p2(UNITS - 1, r)

@@ -1,8 +1,6 @@
 from contextlib import ExitStack
 
-import concourse.bass as bass
 import concourse.mybir as mybir
-import concourse.tile as tile
 from concourse.masks import make_identity
 
 F32 = mybir.dt.float32
@@ -21,44 +19,49 @@ K_IN = 1024
 J_OUT = 512
 PACK = 4
 K_PASS = P * PACK
+PASSES = K_IN // K_PASS
 TILES = 8
 GROUP_ROWS = TILES * P
 GROUPS = ROWS // GROUP_ROWS
-UNITS = 4
-NS = 16
+HALVES = GROUPS * PASSES
+STEPS = BLOCKS * HALVES
 EPS = 1e-5
+ROOT_ROWS = 64.0
 
 FLOPS = 2 * BLOCKS * ROWS * K_IN * J_OUT
 
-S_CHUNKS = (2, 3, 4, 4)
-S_REGROUP = (0, 0, 0, 1024)
-S_NORM = (0, 0, 0, 1)
-XT_BUFS = 10
-W_LOAD_STEP = (1, 7)
-W_PREP_STEP = (5, 10)
+S_PATH = (2, 4)
+BANK_ORDER = (0, 2, 1, 3)
+S_REGROUP = (0, 768)
+BUBBLE = 2
+LOADS_AHEAD = 5
+MANUAL = True
 
 
 def tile_decoder_pa_t_kernel(tc, h6_pre, g6, be6, W7, b7, out):
     nc = tc.nc
     with ExitStack() as ctx:
         const = ctx.enter_context(tc.tile_pool(name="const", bufs=1))
-        natp = ctx.enter_context(tc.tile_pool(name="natp", bufs=4))
-        xtp = ctx.enter_context(tc.tile_pool(name="xtp", bufs=XT_BUFS))
+        natp = ctx.enter_context(tc.tile_pool(name="natp", bufs=5))
+        xtp = ctx.enter_context(tc.tile_pool(name="xtp", bufs=10))
         statp = ctx.enter_context(tc.tile_pool(name="statp", bufs=2))
         plp = ctx.enter_context(tc.tile_pool(name="plp", bufs=2))
         grp = ctx.enter_context(tc.tile_pool(name="grp", bufs=2))
-        acp = ctx.enter_context(tc.tile_pool(name="acp", bufs=2))
-        osbp = ctx.enter_context(tc.tile_pool(name="osbp", bufs=2))
-        wp = ctx.enter_context(tc.tile_pool(name="wp", bufs=1))
+        acp = ctx.enter_context(tc.tile_pool(name="acp", bufs=4))
+        osbp = ctx.enter_context(tc.tile_pool(name="osbp", bufs=3))
         tps = ctx.enter_context(tc.psum_pool(name="tps", bufs=3))
-        sump = ctx.enter_context(tc.psum_pool(name="sump", bufs=2))
-        accp = ctx.enter_context(tc.psum_pool(name="accp", bufs=3))
+        sump = ctx.enter_context(tc.psum_pool(name="sump", bufs=1))
+        accp = ctx.enter_context(tc.psum_pool(name="accp", bufs=4))
+        if MANUAL:
+            ctx.enter_context(tc.manual_schedule())
 
         warm = const.tile([P, 2], F32, name="warm")
         nc.vector.memset(warm[:], 1.0)
-        nc.scalar.activation(out=warm[:, 1:2], in_=warm[:, 0:1], func=ACT.Sqrt)
+        nc.scalar.activation(out=warm[:, 1:2], in_=warm[:, 0:1], func=ACT.Square)
         ident = const.tile([P, P], BF16, name="ident")
         make_identity(nc, ident[:])
+        mhalf = const.tile([P, 2 * PACK], F32, name="mhalf")
+        nc.gpsimd.memset(mhalf[:], -0.5)
         ones = const.tile([P, P], BF16, name="ones")
         nc.vector.memset(ones[:], 1.0)
         rows = const.tile([P, P], BF16, name="rows")
@@ -71,203 +74,281 @@ def tile_decoder_pa_t_kernel(tc, h6_pre, g6, be6, W7, b7, out):
         junk = const.tile([P, GROUP_ROWS], BF16, name="junk")
         gb = const.tile([P, 32], F32, name="gb")
         bias = const.tile([P, BLOCKS, J_OUT], F32, name="bias")
-        wc = const.tile([P, BLOCKS, 2, J_OUT], U32, name="wc", align_bytes=64)
-        ws = const.tile([P, BLOCKS, 2, J_OUT], U8, name="ws", align_bytes=64)
-        ac0 = const.tile([P, ROWS], U32, name="ac0", align_bytes=64)
-        as0 = const.tile([P, ROWS], U8, name="as0", align_bytes=64)
+        wc = const.tile([P, BLOCKS, PASSES * J_OUT], U32, name="wc", align_bytes=64)
+        ws = const.tile([P, BLOCKS, PASSES * J_OUT], U8, name="ws", align_bytes=64)
+
+        def grouped_views(dst, src):
+            return (dst.rearrange("p (c i) t -> p c t i", i=4),
+                    src.rearrange("p t (c i) -> p c t i", i=4))
+
+        nat_of = {}
+        w_nat = {}
+        queue = []
+        for s in range(STEPS):
+            if s == 5:
+                queue.append(("w", 0))
+            if s == 7:
+                queue.append(("w", 1))
+            queue.append(("x", s))
+        issued = [0]
+
+        def next_load():
+            if issued[0] == len(queue):
+                return
+            kind, s = queue[issued[0]]
+            issued[0] = issued[0] + 1
+            if kind == "w":
+                wn = natp.tile([P, 4, K_IN], BF16, name="nat")
+                nc.sync.dma_start(out=wn[:], in_=W7[s].rearrange("(a o) k -> o a k", o=P))
+                w_nat[s] = wn
+                next_load()
+                return
+            b, h = divmod(s, HALVES)
+            r, g = divmod(h, PASSES)
+            nat = natp.tile([P, TILES, K_PASS], BF16, name="nat")
+            nc.sync.dma_start(
+                out=nat[:],
+                in_=h6_pre[b, r * GROUP_ROWS:(r + 1) * GROUP_ROWS, g * K_PASS:(g + 1) * K_PASS]
+                .rearrange("(q t) k -> q t k", t=TILES))
+            nat_of[s] = nat
+
+        for i in range(LOADS_AHEAD):
+            next_load()
 
         def small_params():
-            tp = tps.tile([P, TILES, P], BF16, name="tp")
-            nc.tensor.transpose(tp[:, 0, :], rows[:], ident[:])
-            nc.vector.tensor_copy(out=gb[:], in_=tp[:, 0, 0:32])
+            tp0 = tps.tile([P, TILES, P], BF16, name="tp")
+            nc.tensor.transpose(tp0[:, 0, :], rows[:], ident[:])
+            nc.vector.tensor_scalar(out=gb[:, 0:16], in0=tp0[:, 0, 0:16], scalar1=ROOT_ROWS, scalar2=None,
+                                    op0=ALU.mult)
+            nc.vector.tensor_copy(out=gb[:, 16:32], in_=tp0[:, 0, 16:32])
             for b in range(BLOCKS):
                 acc = accp.tile([P, J_OUT], F32, name="acc")
                 nc.tensor.matmul(out=acc[:], lhsT=ones[:], rhs=brow[:, b * J_OUT:(b + 1) * J_OUT],
                                  start=True, stop=True)
                 nc.vector.tensor_copy(out=bias[:, b, :], in_=acc[:])
 
-        def grouped_views(dst, src):
-            return (dst.rearrange("p (c i) t -> p c t i", i=4),
-                    src.rearrange("p t (c i) -> p c t i", i=4))
-
-        def w_load(b):
-            wn = natp.tile([P, 4, K_IN], BF16, name="nat")
-            nc.sync.dma_start(out=wn[:], in_=W7[b].rearrange("(a o) k -> o a k", o=P))
-            return wn
-
-        def w_prep(b, wn):
-            for g in range(2):
-                wpl = wp.tile([P, PACK, J_OUT], BF16, name="wpl")
-                for h in range(2):
-                    tp = tps.tile([P, TILES, P], BF16, name="tp")
-                    for jj in range(2):
-                        c = g * PACK + 2 * h + jj
-                        for a in range(4):
-                            nc.tensor.transpose(tp[:, jj * 4 + a, :], wn[:, a, c * P:(c + 1) * P], ident[:])
-                    nc.scalar.copy(out=wpl[:, 2 * h:2 * h + 2, :].rearrange("q j o -> q (j o)").bitcast(F32),
-                                   in_=tp[:].rearrange("q t n -> q (t n)").bitcast(F32))
-                wgr = wp.tile([P, J_OUT, PACK], BF16, name="wgr", align_bytes=64)
-                d, s = grouped_views(wgr[:], wpl[:])
-                nc.vector.tensor_copy(out=d, in_=s)
-                nc.vector.quantize_mx(out=wc[:, b, g, :].bitcast(FP8X4), scales=ws[:, b, g, :],
-                                      in_=wgr[:].rearrange("p n t -> p (n t)"))
-
         st = {}
+        xts = {}
 
-        def load(u, r):
-            b, g = divmod(u, 2)
-            nat = natp.tile([P, TILES, K_PASS], BF16, name="nat")
-            nc.sync.dma_start(
-                out=nat[:],
-                in_=h6_pre[b, r * GROUP_ROWS:(r + 1) * GROUP_ROWS, g * K_PASS:(g + 1) * K_PASS]
-                .rearrange("(q t) k -> q t k", t=TILES))
-            return nat
-
-        def p1_open(u):
-            ns = S_CHUNKS[u]
+        def open_block(b):
+            sp = S_PATH[b]
             d = {}
-            d["xt"] = {}
-            if ns > 0:
-                d["sq"] = statp.tile([P, PACK, GROUPS], F32, name="sq")
-                d["sums"] = sump.tile([P, GROUPS * PACK * NS], F32, name="sums")
-            if ns < PACK:
-                d["bst"] = statp.tile([P, PACK, 2 * GROUPS, 6], F32, name="bst")
-            st[u] = d
+            d["sq"] = statp.tile([P, PASSES * sp, GROUPS], F32, name="sq")
+            d["sums"] = sump.tile([P, 512], F32, name="sums")
+            if sp < PACK:
+                d["bst"] = statp.tile([P, PASSES * (PACK - sp), 2 * GROUPS, 6], F32, name="bst")
+            st[b] = d
 
-        def p1(u, r, nat):
-            ns = S_CHUNKS[u]
-            d = st[u]
-            xt = xtp.tile([P, PACK, GROUP_ROWS], BF16, name="xt")
-            d["xt"][r] = xt
-            for j in range(PACK):
-                tp = tps.tile([P, TILES, P], BF16, name="tp")
+        def bank(s, x):
+            b, h = divmod(s, HALVES)
+            r, g = divmod(h, PASSES)
+            sp = S_PATH[b]
+            d = st[b]
+            nat = nat_of[s]
+            xt = xts[s]
+            tp = tps.tile([P, TILES, P], BF16, name="tp")
+            for t in range(TILES):
+                nc.tensor.transpose(tp[:, t, :], nat[:, t, x * P:(x + 1) * P], ident[:])
+            flat = tp[:].rearrange("q t n -> q (t n)")
+            if x < sp:
+                n_sum = 512 // (HALVES * sp)
+                col = (h * sp + x) * n_sum
                 for t in range(TILES):
-                    nc.tensor.transpose(tp[:, t, :], nat[:, t, j * P:(j + 1) * P], ident[:])
-                flat = tp[:].rearrange("q t n -> q (t n)")
-                dst = xt[:, j, :]
-                if j < ns:
-                    col = (r * PACK + j) * NS
-                    for t in range(TILES):
-                        nc.tensor.matmul(out=d["sums"][:, col:col + NS], lhsT=nat[:, t, j * P:(j + 1) * P],
-                                         rhs=ones[:, 0:NS], start=(t == 0), stop=(t == TILES - 1))
-                    nc.scalar.copy(out=dst.bitcast(F32), in_=flat.bitcast(F32))
-                    nc.scalar.activation(out=junk[:], in_=flat, func=ACT.Square, bias=d["xt"][0][:, j, 0:1],
-                                         scale=-1.0, accum_out=d["sq"][:, j, r:r + 1])
-                else:
-                    nc.vector.tensor_copy(out=dst, in_=flat)
-                    for h in range(2):
-                        nc.vector.bn_stats(out=d["bst"][:, j, 2 * r + h, :], in_=flat[:, h * 512:(h + 1) * 512])
+                    nc.tensor.matmul(out=d["sums"][:, col:col + n_sum], lhsT=nat[:, t, x * P:(x + 1) * P],
+                                     rhs=ones[:, 0:n_sum], start=(t == 0), stop=(t == TILES - 1))
+                nc.scalar.copy(out=xt[:, x, :].bitcast(F32), in_=flat.bitcast(F32))
+                nc.scalar.activation(out=junk[:], in_=flat, func=ACT.Square, bias=xts[b * HALVES + g][:, x, 0:1],
+                                     scale=-1.0, accum_out=d["sq"][:, g * sp + x, r:r + 1])
+            else:
+                nc.vector.tensor_copy(out=xt[:, x, :], in_=flat)
+                for hh in range(2):
+                    nc.vector.bn_stats(out=d["bst"][:, g * (PACK - sp) + x - sp, 2 * r + hh, :],
+                                       in_=flat[:, hh * 512:(hh + 1) * 512])
 
-        def fin(u):
-            b, g = divmod(u, 2)
-            ns = S_CHUNKS[u]
-            d = st[u]
-            xt = d["xt"][0]
-            mv = statp.tile([P, PACK, 2], F32, name="mv")
-            if ns > 0:
-                s1 = statp.tile([P, PACK], F32, name="s1")
-                s2 = statp.tile([P, PACK], F32, name="s2")
-                df = statp.tile([P, PACK], F32, name="df")
-                nc.vector.tensor_reduce(
-                    out=s1[:, 0:ns],
-                    in_=d["sums"][:].rearrange("q (r j n) -> q j r n", r=GROUPS, j=PACK)[:, 0:ns, :, 0],
-                    axis=AX.X, op=ALU.add)
-                nc.vector.tensor_reduce(out=s2[:, 0:ns], in_=d["sq"][:, 0:ns, :], axis=AX.X, op=ALU.add)
-                nc.vector.tensor_scalar(out=mv[:, 0:ns, 0], in0=s1[:, 0:ns], scalar1=1.0 / ROWS, scalar2=None,
-                                        op0=ALU.mult)
-                nc.vector.tensor_tensor(out=df[:, 0:ns], in0=mv[:, 0:ns, 0], in1=xt[:, 0:ns, 0], op=ALU.subtract)
-                nc.vector.tensor_tensor(out=df[:, 0:ns], in0=df[:, 0:ns], in1=df[:, 0:ns], op=ALU.mult)
-                nc.vector.scalar_tensor_tensor(out=mv[:, 0:ns, 1], in0=s2[:, 0:ns], scalar=1.0 / ROWS,
-                                               in1=df[:, 0:ns], op0=ALU.mult, op1=ALU.subtract)
-            for j in range(ns, PACK):
-                nc.vector.bn_aggr(out=mv[:, j, :], in_=d["bst"][:, j, :, :].rearrange("q a s -> q (a s)"))
-            ve = statp.tile([P, PACK], F32, name="ve")
-            sd = statp.tile([P, PACK], F32, name="sd")
-            sc = statp.tile([P, PACK], F32, name="sc")
-            bi = statp.tile([P, PACK], F32, name="bi")
-            nc.vector.tensor_scalar(out=ve[:], in0=mv[:, :, 1], scalar1=0.0, scalar2=EPS, op0=ALU.max, op1=ALU.add)
-            nc.scalar.activation(out=sd[:], in_=ve[:], func=ACT.Sqrt)
-            nc.vector.reciprocal(out=ve[:], in_=sd[:])
-            c0 = b * 8 + g * PACK
-            nc.vector.tensor_tensor(out=sc[:], in0=gb[:, c0:c0 + PACK], in1=ve[:], op=ALU.mult)
-            nc.vector.tensor_tensor(out=sd[:], in0=mv[:, :, 0], in1=sc[:], op=ALU.mult)
-            nc.vector.tensor_tensor(out=bi[:], in0=gb[:, 16 + c0:16 + c0 + PACK], in1=sd[:], op=ALU.subtract)
+        def w_transpose(b):
+            wn = w_nat[b]
+            wpl = plp.tile([P, PASSES * PACK, J_OUT], BF16, name="pl")
+            for hb in range(4):
+                tp = tps.tile([P, TILES, P], BF16, name="tp")
+                for jj in range(2):
+                    c = 2 * hb + jj
+                    for a in range(4):
+                        nc.tensor.transpose(tp[:, jj * 4 + a, :], wn[:, a, c * P:(c + 1) * P], ident[:])
+                dst = wpl[:, 2 * hb:2 * hb + 2, :].rearrange("q j o -> q (j o)").bitcast(F32)
+                src = tp[:].rearrange("q t n -> q (t n)").bitcast(F32)
+                if hb % 2 == 0:
+                    nc.scalar.copy(out=dst, in_=src)
+                else:
+                    nc.vector.tensor_copy(out=dst, in_=src)
+            wgr = grp.tile([P, PASSES, J_OUT, PACK], BF16, name="gr", align_bytes=64)
+            for g in range(PASSES):
+                dv, sv = grouped_views(wgr[:, g, :, :], wpl[:, g * PACK:(g + 1) * PACK, :])
+                nc.gpsimd.tensor_scalar(out=dv, in0=sv, scalar1=1.0, scalar2=0.0, op0=ALU.mult, op1=ALU.add)
+            return wgr
+
+        def w_quantise(b, wgr):
+            nc.vector.quantize_mx(out=wc[:, b, :].bitcast(FP8X4), scales=ws[:, b, :],
+                                  in_=wgr[:].rearrange("p g n t -> p (g n t)"))
+
+        def finish_stats(b):
+            sp = S_PATH[b]
+            d = st[b]
+            w = PASSES * sp
+            s1 = statp.tile([P, PASSES, sp], F32, name="s1")
+            s2 = statp.tile([P, PASSES, sp], F32, name="s2")
+            df = statp.tile([P, PASSES, sp], F32, name="df")
+            mean = statp.tile([P, PASSES, PACK], F32, name="mean")
+            varn = statp.tile([P, PASSES, PACK], F32, name="varn")
+            rs = statp.tile([P, PASSES * PACK], F32, name="rs")
+            sc = statp.tile([P, PASSES * PACK], F32, name="sc")
+            bi = statp.tile([P, PASSES * PACK], F32, name="bi")
+            nc.vector.tensor_reduce(
+                out=s1[:].rearrange("q g x -> q (g x)"),
+                in_=d["sums"][:].rearrange("q (r c n) -> q c r n", r=GROUPS, c=w)[:, :, :, 0],
+                axis=AX.X, op=ALU.add)
+            nc.gpsimd.tensor_scalar(out=mean[:, :, 0:sp], in0=s1[:], scalar1=1.0 / ROWS, scalar2=0.0,
+                                    op0=ALU.mult, op1=ALU.add)
+            for g in range(PASSES):
+                nc.gpsimd.tensor_tensor(out=df[:, g, :], in0=mean[:, g, 0:sp], in1=xts[b * HALVES + g][:, 0:sp, 0],
+                                        op=ALU.subtract)
+            nc.gpsimd.tensor_scalar(out=s1[:], in0=df[:], scalar1=float(ROWS), scalar2=0.0, op0=ALU.mult, op1=ALU.add)
+            nc.gpsimd.tensor_tensor(out=df[:], in0=df[:], in1=s1[:], op=ALU.mult)
+            if sp < PACK:
+                mvv = statp.tile([P, PASSES, PACK - sp, 2], F32, name="mvv")
+                for g in range(PASSES):
+                    for x in range(PACK - sp):
+                        nc.vector.bn_aggr(out=mvv[:, g, x, :],
+                                          in_=d["bst"][:, g * (PACK - sp) + x, :, :].rearrange("q a s -> q (a s)"))
+                nc.gpsimd.tensor_scalar(out=mean[:, :, sp:PACK], in0=mvv[:, :, :, 0], scalar1=1.0, scalar2=0.0,
+                                        op0=ALU.mult, op1=ALU.add)
+                nc.gpsimd.tensor_scalar(out=varn[:, :, sp:PACK], in0=mvv[:, :, :, 1], scalar1=float(ROWS), scalar2=0.0,
+                                        op0=ALU.mult, op1=ALU.add)
+            nc.vector.tensor_reduce(out=s2[:].rearrange("q g x -> q (g x)"), in_=d["sq"][:], axis=AX.X, op=ALU.add)
+            nc.gpsimd.tensor_tensor(out=varn[:, :, 0:sp], in0=s2[:], in1=df[:], op=ALU.subtract)
+            flat_var = varn[:].rearrange("q g x -> q (g x)")
+            flat_mean = mean[:].rearrange("q g x -> q (g x)")
+            nc.gpsimd.tensor_scalar(out=rs[:], in0=flat_var, scalar1=0.0, scalar2=EPS * ROWS, op0=ALU.max, op1=ALU.add)
+            nc.gpsimd.tensor_tensor(out=rs[:], in0=rs[:], in1=mhalf[:], op=ALU.pow)
+            nc.gpsimd.tensor_tensor(out=sc[:], in0=gb[:, b * 8:b * 8 + 8], in1=rs[:], op=ALU.mult)
+            nc.gpsimd.tensor_tensor(out=rs[:], in0=flat_mean, in1=sc[:], op=ALU.mult)
+            nc.gpsimd.tensor_tensor(out=bi[:], in0=gb[:, 16 + b * 8:16 + b * 8 + 8], in1=rs[:], op=ALU.subtract)
             d["sc"] = sc
             d["bi"] = bi
 
-        def p2(u, r):
-            b, g = divmod(u, 2)
-            d = st[u]
-            xt = d["xt"][r]
+        work = {}
+
+        def norms(s):
+            b, h = divmod(s, HALVES)
+            g = h % PASSES
+            d = st[b]
+            xt = xts[s]
             pl = plp.tile([P, PACK, GROUP_ROWS], BF16, name="pl")
-            for j in range(PACK):
-                if j < PACK - S_NORM[u]:
-                    nc.vector.tensor_scalar(out=pl[:, j, :], in0=xt[:, j, :],
-                                            scalar1=d["sc"][:, j:j + 1], scalar2=d["bi"][:, j:j + 1],
-                                            op0=ALU.mult, op1=ALU.add)
-                else:
-                    nc.scalar.activation(out=pl[:, j, :], in_=xt[:, j, :], func=ACT.Relu,
-                                         bias=d["bi"][:, j:j + 1], scale=d["sc"][:, j:j + 1])
+            for x in range(PACK):
+                c = g * PACK + x
+                nc.vector.tensor_scalar(out=pl[:, x, :], in0=xt[:, x, :], scalar1=d["sc"][:, c:c + 1],
+                                        scalar2=d["bi"][:, c:c + 1], op0=ALU.mult, op1=ALU.add)
+            work[s] = {"pl": pl}
+
+        def regroup(s):
+            b = s // HALVES
+            pl = work[s]["pl"]
             gr = grp.tile([P, GROUP_ROWS, PACK], BF16, name="gr", align_bytes=64)
-            cv = GROUP_ROWS - S_REGROUP[u]
-            if cv > 0:
-                dv, sv = grouped_views(gr[:, 0:cv, :], pl[:, :, 0:cv])
-                nc.vector.tensor_scalar(out=dv, in0=sv, scalar1=0.0, scalar2=None, op0=ALU.max)
+            cv = GROUP_ROWS - S_REGROUP[b]
             if cv < GROUP_ROWS:
                 da, sa = grouped_views(gr[:, cv:GROUP_ROWS, :], pl[:, :, cv:GROUP_ROWS])
                 nc.scalar.activation(out=da, in_=sa, func=ACT.Relu)
-            if g == 0:
-                codes = ac0[:, r * GROUP_ROWS:(r + 1) * GROUP_ROWS]
-                scales = as0[:, r * GROUP_ROWS:(r + 1) * GROUP_ROWS]
-            else:
-                ac1 = acp.tile([P, GROUP_ROWS], U32, name="ac1", align_bytes=64)
-                as1 = acp.tile([P, GROUP_ROWS], U8, name="as1", align_bytes=64)
-                codes = ac1[:]
-                scales = as1[:]
-            nc.vector.quantize_mx(out=codes.bitcast(FP8X4), scales=scales,
-                                  in_=gr[:].rearrange("p n t -> p (n t)"))
-            if g == 0:
-                return
-            dram = out[b, r * GROUP_ROWS:(r + 1) * GROUP_ROWS, :].rearrange("(q t) j -> q t j", t=TILES)
-            for h in range(2):
-                osb = osbp.tile([P, 4, J_OUT], F32, name="osb")
-                for tt in range(4):
-                    t = 4 * h + tt
-                    c0 = r * GROUP_ROWS + t * P
-                    acc = accp.tile([P, J_OUT], F32, name="acc")
-                    nc.tensor.matmul_mx(out=acc[:], lhsT=ac0[:, c0:c0 + P].bitcast(FP8X4),
-                                        lhsT_scale=as0[:, c0:c0 + P],
-                                        rhs=wc[:, b, 0, :].bitcast(FP8X4), rhs_scale=ws[:, b, 0, :],
-                                        start=True, stop=False)
-                    nc.tensor.matmul_mx(out=acc[:], lhsT=codes[:, t * P:(t + 1) * P].bitcast(FP8X4),
-                                        lhsT_scale=scales[:, t * P:(t + 1) * P],
-                                        rhs=wc[:, b, 1, :].bitcast(FP8X4), rhs_scale=ws[:, b, 1, :],
-                                        start=False, stop=True)
-                    nc.vector.tensor_tensor(out=osb[:, tt, :], in0=acc[:], in1=bias[:, b, :], op=ALU.add)
-                nc.sync.dma_start(out=dram[:, 4 * h:4 * h + 4, :], in_=osb[:])
+            dv, sv = grouped_views(gr[:, 0:cv, :], pl[:, :, 0:cv])
+            nc.vector.tensor_scalar(out=dv, in0=sv, scalar1=0.0, scalar2=None, op0=ALU.max)
+            work[s]["gr"] = gr
 
-        steps = [(u, r) for u in range(UNITS) for r in range(GROUPS)]
-        ahead = 4
-        nats = {}
-        wns = {}
-        for s in range(ahead):
-            nats[s] = load(steps[s][0], steps[s][1])
-        small_params()
-        for s in range(len(steps)):
-            u, r = steps[s]
-            if r == 0:
-                p1_open(u)
-            p1(u, r, nats[s])
-            if s + ahead < len(steps):
-                nats[s + ahead] = load(steps[s + ahead][0], steps[s + ahead][1])
-            for b in range(BLOCKS):
-                if s == W_LOAD_STEP[b]:
-                    wns[b] = w_load(b)
-                if s == W_PREP_STEP[b]:
-                    w_prep(b, wns[b])
-            if u >= 1:
-                p2(u - 1, r)
-            if r == GROUPS - 1:
-                fin(u)
-        for r in range(GROUPS):
-            p2(UNITS - 1, r)
+        def quantise(s):
+            codes = acp.tile([P, GROUP_ROWS], U32, name="codes", align_bytes=64)
+            scales = acp.tile([P, GROUP_ROWS], U8, name="scales", align_bytes=64)
+            nc.vector.quantize_mx(out=codes[:].bitcast(FP8X4), scales=scales[:],
+                                  in_=work[s]["gr"][:].rearrange("p n t -> p (n t)"))
+            work[s]["codes"] = codes
+            work[s]["scales"] = scales
+
+        def multiply(m, hb):
+            b = m // GROUPS
+            accs = []
+            for tt in range(4):
+                t = 4 * hb + tt
+                acc = accp.tile([P, J_OUT], F32, name="acc")
+                for g in range(PASSES):
+                    wk = work[PASSES * m + g]
+                    nc.tensor.matmul_mx(out=acc[:], lhsT=wk["codes"][:, t * P:(t + 1) * P].bitcast(FP8X4),
+                                        lhsT_scale=wk["scales"][:, t * P:(t + 1) * P],
+                                        rhs=wc[:, b, g * J_OUT:(g + 1) * J_OUT].bitcast(FP8X4),
+                                        rhs_scale=ws[:, b, g * J_OUT:(g + 1) * J_OUT],
+                                        start=(g == 0), stop=(g == PASSES - 1))
+                accs.append(acc)
+            work[("acc", m, hb)] = accs
+
+        def add_bias_and_store(m, hb):
+            b, r = divmod(m, GROUPS)
+            accs = work[("acc", m, hb)]
+            osb = osbp.tile([P, 4, J_OUT], F32, name="osb")
+            for tt in range(4):
+                nc.vector.tensor_tensor(out=osb[:, tt, :], in0=accs[tt][:], in1=bias[:, b, :], op=ALU.add)
+            dram = out[b, r * GROUP_ROWS:(r + 1) * GROUP_ROWS, :].rearrange("(q t) j -> q t j", t=TILES)
+            nc.sync.dma_start(out=dram[:, 4 * hb:4 * hb + 4, :], in_=osb[:])
+
+        open_block(0)
+        wgrs = {}
+        for s in range(HALVES):
+            xts[s] = xtp.tile([P, PACK, GROUP_ROWS], BF16, name="xt")
+            for x in BANK_ORDER:
+                bank(s, x)
+            next_load()
+            if s == 3:
+                small_params()
+            if s == 4:
+                wgrs[0] = w_transpose(0)
+            if s == 6:
+                wgrs[1] = w_transpose(1)
+        finish_stats(0)
+        w_quantise(0, wgrs[0])
+        w_quantise(1, wgrs[1])
+        open_block(1)
+
+        def slot_of(s):
+            return s + (BUBBLE if s >= HALVES else 0)
+
+        quantise_at = {}
+        norm_at = {}
+        multiply_at = {}
+        store_at = {}
+        for s in range(STEPS):
+            quantise_at[slot_of(s)] = s
+            norm_at[slot_of(s) - 1] = s
+        for m in range(BLOCKS * GROUPS):
+            for hb in range(2):
+                multiply_at[slot_of(PASSES * m + 1) + hb] = (m, hb)
+                store_at[slot_of(PASSES * m + 1) + hb + 1] = (m, hb)
+
+        norms(0)
+        regroup(0)
+        for q in range(slot_of(STEPS - 1) + 3):
+            s1 = HALVES + q
+            first = q < HALVES
+            if first:
+                xts[s1] = xtp.tile([P, PACK, GROUP_ROWS], BF16, name="xt")
+                bank(s1, 0)
+                bank(s1, 1)
+            if q in norm_at:
+                norms(norm_at[q])
+            if q in quantise_at:
+                quantise(quantise_at[q])
+            if q in store_at:
+                add_bias_and_store(store_at[q][0], store_at[q][1])
+            if first:
+                bank(s1, 2)
+                bank(s1, 3)
+                next_load()
+            if q in multiply_at:
+                multiply(multiply_at[q][0], multiply_at[q][1])
+            if q in norm_at:
+                regroup(norm_at[q])
+            if q == HALVES - 1:
+                finish_stats(1)

@@ -35,6 +35,7 @@ BANK_ORDER = (0, 2, 1, 3)
 S_REGROUP = (0, 768)
 BUBBLE = 2
 LOADS_AHEAD = 5
+WIDE_SUMS = (True, False)
 MANUAL = True
 
 
@@ -134,7 +135,10 @@ def tile_decoder_pa_t_kernel(tc, h6_pre, g6, be6, W7, b7, out):
             sp = S_PATH[b]
             d = {}
             d["sq"] = statp.tile([P, PASSES * sp, GROUPS], F32, name="sq")
-            d["sums"] = sump.tile([P, 512], F32, name="sums")
+            if WIDE_SUMS[b]:
+                d["part"] = statp.tile([P, PASSES * sp, GROUPS], F32, name="part")
+            else:
+                d["sums"] = sump.tile([P, 512], F32, name="sums")
             if sp < PACK:
                 d["bst"] = statp.tile([P, PASSES * (PACK - sp), 2 * GROUPS, 6], F32, name="bst")
             st[b] = d
@@ -151,8 +155,14 @@ def tile_decoder_pa_t_kernel(tc, h6_pre, g6, be6, W7, b7, out):
                 nc.tensor.transpose(tp[:, t, :], nat[:, t, x * P:(x + 1) * P], ident[:])
             flat = tp[:].rearrange("q t n -> q (t n)")
             if x < sp:
-                n_sum = 512 // (HALVES * sp)
-                col = (h * sp + x) * n_sum
+                if WIDE_SUMS[b]:
+                    n_sum = 512 // (PASSES * sp)
+                    col = (g * sp + x) * n_sum
+                    if col == 0:
+                        d["sums"] = accp.tile([P, 512], F32, name="acc")
+                else:
+                    n_sum = 512 // (HALVES * sp)
+                    col = (h * sp + x) * n_sum
                 for t in range(TILES):
                     nc.tensor.matmul(out=d["sums"][:, col:col + n_sum], lhsT=nat[:, t, x * P:(x + 1) * P],
                                      rhs=ones[:, 0:n_sum], start=(t == 0), stop=(t == TILES - 1))
@@ -202,10 +212,13 @@ def tile_decoder_pa_t_kernel(tc, h6_pre, g6, be6, W7, b7, out):
             rs = statp.tile([P, PASSES * PACK], F32, name="rs")
             sc = statp.tile([P, PASSES * PACK], F32, name="sc")
             bi = statp.tile([P, PASSES * PACK], F32, name="bi")
-            nc.vector.tensor_reduce(
-                out=s1[:].rearrange("q g x -> q (g x)"),
-                in_=d["sums"][:].rearrange("q (r c n) -> q c r n", r=GROUPS, c=w)[:, :, :, 0],
-                axis=AX.X, op=ALU.add)
+            if WIDE_SUMS[b]:
+                nc.vector.tensor_reduce(out=s1[:].rearrange("q g x -> q (g x)"), in_=d["part"][:], axis=AX.X, op=ALU.add)
+            else:
+                nc.vector.tensor_reduce(
+                    out=s1[:].rearrange("q g x -> q (g x)"),
+                    in_=d["sums"][:].rearrange("q (r c n) -> q c r n", r=GROUPS, c=w)[:, :, :, 0],
+                    axis=AX.X, op=ALU.add)
             nc.gpsimd.tensor_scalar(out=mean[:, :, 0:sp], in0=s1[:], scalar1=1.0 / ROWS, scalar2=0.0,
                                     op0=ALU.mult, op1=ALU.add)
             for g in range(PASSES):
@@ -300,6 +313,9 @@ def tile_decoder_pa_t_kernel(tc, h6_pre, g6, be6, W7, b7, out):
             xts[s] = xtp.tile([P, PACK, GROUP_ROWS], BF16, name="xt")
             for x in BANK_ORDER:
                 bank(s, x)
+            if WIDE_SUMS[0] and s % PASSES == PASSES - 1:
+                nc.vector.tensor_copy(out=st[0]["part"][:, :, s // PASSES],
+                                      in_=st[0]["sums"][:].rearrange("q (c n) -> q c n", c=PASSES * S_PATH[0])[:, :, 0])
             next_load()
             if s == 3:
                 small_params()

@@ -32,7 +32,7 @@ FLOPS = 2 * BLOCKS * ROWS * K_IN * J_OUT
 
 S_PATH = (2, 4)
 BANK_ORDER = (0, 2, 1, 3)
-S_REGROUP = (0, 768)
+PRE = 1
 BUBBLE = 2
 LOADS_AHEAD = 5
 WIDE_SUMS = (True, False)
@@ -46,8 +46,8 @@ def tile_decoder_pa_t_kernel(tc, h6_pre, g6, be6, W7, b7, out):
         natp = ctx.enter_context(tc.tile_pool(name="natp", bufs=5))
         xtp = ctx.enter_context(tc.tile_pool(name="xtp", bufs=10))
         statp = ctx.enter_context(tc.tile_pool(name="statp", bufs=2))
-        plp = ctx.enter_context(tc.tile_pool(name="plp", bufs=2))
-        grp = ctx.enter_context(tc.tile_pool(name="grp", bufs=2))
+        plp = ctx.enter_context(tc.tile_pool(name="plp", bufs=3))
+        grp = ctx.enter_context(tc.tile_pool(name="grp", bufs=3))
         acp = ctx.enter_context(tc.tile_pool(name="acp", bufs=4))
         osbp = ctx.enter_context(tc.tile_pool(name="osbp", bufs=3))
         tps = ctx.enter_context(tc.psum_pool(name="tps", bufs=3))
@@ -86,9 +86,9 @@ def tile_decoder_pa_t_kernel(tc, h6_pre, g6, be6, W7, b7, out):
         w_nat = {}
         queue = []
         for s in range(STEPS):
-            if s == 5:
+            if s == 3:
                 queue.append(("w", 0))
-            if s == 7:
+            if s == 5:
                 queue.append(("w", 1))
             queue.append(("x", s))
         issued = [0]
@@ -143,7 +143,7 @@ def tile_decoder_pa_t_kernel(tc, h6_pre, g6, be6, W7, b7, out):
                 d["bst"] = statp.tile([P, PASSES * (PACK - sp), 2 * GROUPS, 6], F32, name="bst")
             st[b] = d
 
-        def bank(s, x):
+        def bank(s, x, vector_copies=False):
             b, h = divmod(s, HALVES)
             r, g = divmod(h, PASSES)
             sp = S_PATH[b]
@@ -166,7 +166,11 @@ def tile_decoder_pa_t_kernel(tc, h6_pre, g6, be6, W7, b7, out):
                 for t in range(TILES):
                     nc.tensor.matmul(out=d["sums"][:, col:col + n_sum], lhsT=nat[:, t, x * P:(x + 1) * P],
                                      rhs=ones[:, 0:n_sum], start=(t == 0), stop=(t == TILES - 1))
-                nc.scalar.copy(out=xt[:, x, :].bitcast(F32), in_=flat.bitcast(F32))
+                if vector_copies:
+                    nc.vector.tensor_copy(out=xt[:, x, :], in_=flat)
+                    flat = xt[:, x, :]
+                else:
+                    nc.scalar.copy(out=xt[:, x, :].bitcast(F32), in_=flat.bitcast(F32))
                 nc.scalar.activation(out=junk[:], in_=flat, func=ACT.Square, bias=xts[b * HALVES + g][:, x, 0:1],
                                      scale=-1.0, accum_out=d["sq"][:, g * sp + x, r:r + 1])
             else:
@@ -266,12 +270,15 @@ def tile_decoder_pa_t_kernel(tc, h6_pre, g6, be6, W7, b7, out):
             b = s // HALVES
             pl = work[s]["pl"]
             gr = grp.tile([P, GROUP_ROWS, PACK], BF16, name="gr", align_bytes=64)
-            cv = GROUP_ROWS - S_REGROUP[b]
+            cv = GROUP_ROWS
+            if b == 1:
+                cv = 512 if s == HALVES else 0
             if cv < GROUP_ROWS:
                 da, sa = grouped_views(gr[:, cv:GROUP_ROWS, :], pl[:, :, cv:GROUP_ROWS])
                 nc.scalar.activation(out=da, in_=sa, func=ACT.Relu)
-            dv, sv = grouped_views(gr[:, 0:cv, :], pl[:, :, 0:cv])
-            nc.vector.tensor_scalar(out=dv, in0=sv, scalar1=0.0, scalar2=None, op0=ALU.max)
+            if cv > 0:
+                dv, sv = grouped_views(gr[:, 0:cv, :], pl[:, :, 0:cv])
+                nc.vector.tensor_scalar(out=dv, in0=sv, scalar1=0.0, scalar2=None, op0=ALU.max)
             work[s]["gr"] = gr
 
         def quantise(s):
@@ -319,13 +326,11 @@ def tile_decoder_pa_t_kernel(tc, h6_pre, g6, be6, W7, b7, out):
             next_load()
             if s == 3:
                 small_params()
-            if s == 4:
+            if s == 2:
                 wgrs[0] = w_transpose(0)
-            if s == 6:
+            if s == 4:
                 wgrs[1] = w_transpose(1)
         finish_stats(0)
-        w_quantise(0, wgrs[0])
-        w_quantise(1, wgrs[1])
         open_block(1)
 
         def slot_of(s):
@@ -335,25 +340,37 @@ def tile_decoder_pa_t_kernel(tc, h6_pre, g6, be6, W7, b7, out):
         norm_at = {}
         multiply_at = {}
         store_at = {}
+        for q in range(-1, slot_of(STEPS - 1) + 3):
+            norm_at[q] = []
         for s in range(STEPS):
             quantise_at[slot_of(s)] = s
-            norm_at[slot_of(s) - 1] = s
+            if s < HALVES:
+                norm_at[slot_of(s) - 1].append(s)
+            else:
+                norm_at[max(slot_of(s) - 2, slot_of(HALVES) - 1)].append(s)
         for m in range(BLOCKS * GROUPS):
             for hb in range(2):
                 multiply_at[slot_of(PASSES * m + 1) + hb] = (m, hb)
                 store_at[slot_of(PASSES * m + 1) + hb + 1] = (m, hb)
 
+        for s in range(HALVES, HALVES + PRE):
+            xts[s] = xtp.tile([P, PACK, GROUP_ROWS], BF16, name="xt")
+            for x in range(PACK):
+                bank(s, x, True)
+            next_load()
+        w_quantise(0, wgrs[0])
+        w_quantise(1, wgrs[1])
         norms(0)
         regroup(0)
         for q in range(slot_of(STEPS - 1) + 3):
-            s1 = HALVES + q
-            first = q < HALVES
+            s1 = HALVES + PRE + q
+            first = s1 < STEPS
             if first:
                 xts[s1] = xtp.tile([P, PACK, GROUP_ROWS], BF16, name="xt")
                 bank(s1, 0)
                 bank(s1, 1)
-            if q in norm_at:
-                norms(norm_at[q])
+            for s in norm_at[q]:
+                norms(s)
             if q in quantise_at:
                 quantise(quantise_at[q])
             if q in store_at:
@@ -364,7 +381,7 @@ def tile_decoder_pa_t_kernel(tc, h6_pre, g6, be6, W7, b7, out):
                 next_load()
             if q in multiply_at:
                 multiply(multiply_at[q][0], multiply_at[q][1])
-            if q in norm_at:
-                regroup(norm_at[q])
-            if q == HALVES - 1:
+            for s in norm_at[q]:
+                regroup(s)
+            if s1 == STEPS - 1:
                 finish_stats(1)

@@ -37,6 +37,7 @@ BUBBLE = 2
 LOADS_AHEAD = 5
 WIDE_SUMS = (True, False)
 MANUAL = True
+V_ROWS_BLOCK1 = 128
 
 
 def tile_decoder_pa_t_kernel(tc, h6_pre, g6, be6, W7, b7, out):
@@ -196,8 +197,8 @@ def tile_decoder_pa_t_kernel(tc, h6_pre, g6, be6, W7, b7, out):
                     nc.vector.tensor_copy(out=dst, in_=src)
             wgr = grp.tile([P, PASSES, J_OUT, PACK], BF16, name="gr", align_bytes=64)
             for g in range(PASSES):
-                dv, sv = grouped_views(wgr[:, g, :, :], wpl[:, g * PACK:(g + 1) * PACK, :])
-                nc.gpsimd.tensor_scalar(out=dv, in0=sv, scalar1=1.0, scalar2=0.0, op0=ALU.mult, op1=ALU.add)
+                nc.gpsimd.tensor_scalar(out=wgr[:, g, :, :], in0=wpl[:, g * PACK:(g + 1) * PACK, :].rearrange("p t n -> p n t"),
+                                        scalar1=1.0, scalar2=0.0, op0=ALU.mult, op1=ALU.add)
             return wgr
 
         def w_quantise(b, wgr):
@@ -272,7 +273,7 @@ def tile_decoder_pa_t_kernel(tc, h6_pre, g6, be6, W7, b7, out):
             gr = grp.tile([P, GROUP_ROWS, PACK], BF16, name="gr", align_bytes=64)
             cv = GROUP_ROWS
             if b == 1:
-                cv = 512 if s == HALVES else 0
+                cv = 512 if s == HALVES else V_ROWS_BLOCK1
             if cv < GROUP_ROWS:
                 da, sa = grouped_views(gr[:, cv:GROUP_ROWS, :], pl[:, :, cv:GROUP_ROWS])
                 nc.scalar.activation(out=da, in_=sa, func=ACT.Relu)

@@ -87,11 +87,10 @@ def tile_decoder_pa_t_kernel(tc, h6_pre, g6, be6, W7, b7, out):
         w_nat = {}
         queue = []
         for s in range(STEPS):
-            if s == 3:
+            if s == HALVES:
                 queue.append(("w", 0))
-            if s == 5:
-                queue.append(("w", 1))
             queue.append(("x", s))
+        queue.append(("w", 1))
         issued = [0]
 
         def next_load():
@@ -191,7 +190,7 @@ def tile_decoder_pa_t_kernel(tc, h6_pre, g6, be6, W7, b7, out):
                         nc.tensor.transpose(tp[:, jj * 4 + a, :], wn[:, a, c * P:(c + 1) * P], ident[:])
                 dst = wpl[:, 2 * hb:2 * hb + 2, :].rearrange("q j o -> q (j o)").bitcast(F32)
                 src = tp[:].rearrange("q t n -> q (t n)").bitcast(F32)
-                if hb % 2 == 0:
+                if hb % 2 == 0 or b == 1:
                     nc.scalar.copy(out=dst, in_=src)
                 else:
                     nc.vector.tensor_copy(out=dst, in_=src)
@@ -327,11 +326,8 @@ def tile_decoder_pa_t_kernel(tc, h6_pre, g6, be6, W7, b7, out):
             next_load()
             if s == 3:
                 small_params()
-            if s == 2:
-                wgrs[0] = w_transpose(0)
-            if s == 4:
-                wgrs[1] = w_transpose(1)
         finish_stats(0)
+        wgrs[0] = w_transpose(0)
         open_block(1)
 
         def slot_of(s):
@@ -359,8 +355,6 @@ def tile_decoder_pa_t_kernel(tc, h6_pre, g6, be6, W7, b7, out):
             for x in range(PACK):
                 bank(s, x, True)
             next_load()
-        w_quantise(0, wgrs[0])
-        w_quantise(1, wgrs[1])
         norms(0)
         regroup(0)
         for q in range(slot_of(STEPS - 1) + 3):
@@ -374,6 +368,10 @@ def tile_decoder_pa_t_kernel(tc, h6_pre, g6, be6, W7, b7, out):
                 norms(s)
             if q in quantise_at:
                 quantise(quantise_at[q])
+            if q == 0:
+                w_quantise(0, wgrs[0])
+            if q == slot_of(HALVES):
+                w_quantise(1, wgrs[1])
             if q in store_at:
                 add_bias_and_store(store_at[q][0], store_at[q][1])
             if first:
@@ -386,3 +384,4 @@ def tile_decoder_pa_t_kernel(tc, h6_pre, g6, be6, W7, b7, out):
                 regroup(s)
             if s1 == STEPS - 1:
                 finish_stats(1)
+                wgrs[1] = w_transpose(1)

@@ -181,23 +181,20 @@ def tile_decoder_pa_t_kernel(tc, h6_pre, g6, be6, W7, b7, out):
 
         def w_transpose(b):
             wn = w_nat[b]
-            wpl = plp.tile([P, PASSES * PACK, J_OUT], BF16, name="pl")
-            for hb in range(4):
-                tp = tps.tile([P, TILES, P], BF16, name="tp")
-                for jj in range(2):
-                    c = 2 * hb + jj
-                    for a in range(4):
-                        nc.tensor.transpose(tp[:, jj * 4 + a, :], wn[:, a, c * P:(c + 1) * P], ident[:])
-                dst = wpl[:, 2 * hb:2 * hb + 2, :].rearrange("q j o -> q (j o)").bitcast(F32)
-                src = tp[:].rearrange("q t n -> q (t n)").bitcast(F32)
-                if hb % 2 == 0 or b == 1:
-                    nc.scalar.copy(out=dst, in_=src)
-                else:
-                    nc.vector.tensor_copy(out=dst, in_=src)
             wgr = grp.tile([P, PASSES, J_OUT, PACK], BF16, name="gr", align_bytes=64)
             for g in range(PASSES):
-                nc.gpsimd.tensor_scalar(out=wgr[:, g, :, :], in0=wpl[:, g * PACK:(g + 1) * PACK, :].rearrange("p t n -> p n t"),
-                                        scalar1=1.0, scalar2=0.0, op0=ALU.mult, op1=ALU.add)
+                for h in range(2):
+                    tp = tps.tile([P, TILES, P], BF16, name="tp")
+                    for t in range(PACK):
+                        for a in range(2):
+                            c = g * PACK + t
+                            nc.tensor.transpose(tp[:, 2 * t + a, :], wn[:, 2 * h + a, c * P:(c + 1) * P], ident[:])
+                    dst = wgr[:, g, 256 * h:256 * (h + 1), :].rearrange("p (a j) t -> p a j t", a=2)
+                    src = tp[:].rearrange("p (t a) j -> p a j t", a=2)
+                    if b == 0:
+                        nc.vector.tensor_copy(out=dst, in_=src)
+                    else:
+                        nc.scalar.copy(out=dst, in_=src)
             return wgr
 
         def w_quantise(b, wgr):

@@ -37,7 +37,8 @@ BUBBLE = 2
 LOADS_AHEAD = 5
 WIDE_SUMS = (True, False)
 MANUAL = True
-V_ROWS_BLOCK1 = 128
+V_ROWS_BLOCK1 = 64
+WARM_UP = 28
 
 
 def tile_decoder_pa_t_kernel(tc, h6_pre, g6, be6, W7, b7, out):
@@ -115,6 +116,10 @@ def tile_decoder_pa_t_kernel(tc, h6_pre, g6, be6, W7, b7, out):
 
         for i in range(LOADS_AHEAD):
             next_load()
+
+        warm_acc = accp.tile([P, J_OUT], F32, name="acc")
+        for i in range(WARM_UP):
+            nc.tensor.matmul(out=warm_acc[:, 0:P], lhsT=ones[:], rhs=ones[:], start=True, stop=True)
 
         def small_params():
             tp0 = tps.tile([P, TILES, P], BF16, name="tp")

@@ -39,6 +39,7 @@ WIDE_SUMS = (True, False)
 MANUAL = True
 V_ROWS_BLOCK1 = 64
 WARM_UP = 28
+RUN = 8
 
 
 def tile_decoder_pa_t_kernel(tc, h6_pre, g6, be6, W7, b7, out):
@@ -81,8 +82,8 @@ def tile_decoder_pa_t_kernel(tc, h6_pre, g6, be6, W7, b7, out):
         ws = const.tile([P, BLOCKS, PASSES * J_OUT], U8, name="ws", align_bytes=64)
 
         def grouped_views(dst, src):
-            return (dst.rearrange("p (c i) t -> p c t i", i=4),
-                    src.rearrange("p t (c i) -> p c t i", i=4))
+            return (dst.rearrange("p (c i) t -> p c t i", i=RUN),
+                    src.rearrange("p t (c i) -> p c t i", i=RUN))
 
         nat_of = {}
         w_nat = {}

from contextlib import ExitStack

import concourse.mybir as mybir
from concourse.masks import make_identity

F32 = mybir.dt.float32
BF16 = mybir.dt.bfloat16
U32 = mybir.dt.uint32
U8 = mybir.dt.uint8
FP8X4 = mybir.dt.float8_e4m3fn_x4
ALU = mybir.AluOpType
ACT = mybir.ActivationFunctionType
AX = mybir.AxisListType

P = 128
BLOCKS = 2
ROWS = 4096
K_IN = 1024
J_OUT = 512
PACK = 4
K_PASS = P * PACK
PASSES = K_IN // K_PASS
TILES = 8
GROUP_ROWS = TILES * P
GROUPS = ROWS // GROUP_ROWS
HALVES = GROUPS * PASSES
STEPS = BLOCKS * HALVES
EPS = 1e-5
ROOT_ROWS = 64.0

FLOPS = 2 * BLOCKS * ROWS * K_IN * J_OUT

S_PATH = (2, 4)
BANK_ORDER = (0, 2, 1, 3)
PRE = 1
BUBBLE = 2
LOADS_AHEAD = 5
WIDE_SUMS = (True, False)
MANUAL = True
V_ROWS_BLOCK1 = 64
WARM_UP = 28
RUN = 8


def tile_decoder_pa_t_kernel(tc, h6_pre, g6, be6, W7, b7, out):
    nc = tc.nc
    with ExitStack() as ctx:
        const = ctx.enter_context(tc.tile_pool(name="const", bufs=1))
        natp = ctx.enter_context(tc.tile_pool(name="natp", bufs=5))
        xtp = ctx.enter_context(tc.tile_pool(name="xtp", bufs=10))
        statp = ctx.enter_context(tc.tile_pool(name="statp", bufs=2))
        plp = ctx.enter_context(tc.tile_pool(name="plp", bufs=3))
        grp = ctx.enter_context(tc.tile_pool(name="grp", bufs=3))
        acp = ctx.enter_context(tc.tile_pool(name="acp", bufs=4))
        osbp = ctx.enter_context(tc.tile_pool(name="osbp", bufs=3))
        tps = ctx.enter_context(tc.psum_pool(name="tps", bufs=3))
        sump = ctx.enter_context(tc.psum_pool(name="sump", bufs=1))
        accp = ctx.enter_context(tc.psum_pool(name="accp", bufs=4))
        if MANUAL:
            ctx.enter_context(tc.manual_schedule())

        warm = const.tile([P, 2], F32, name="warm")
        nc.vector.memset(warm[:], 1.0)
        nc.scalar.activation(out=warm[:, 1:2], in_=warm[:, 0:1], func=ACT.Square)
        ident = const.tile([P, P], BF16, name="ident")
        make_identity(nc, ident[:])
        mhalf = const.tile([P, 2 * PACK], F32, name="mhalf")
        nc.gpsimd.memset(mhalf[:], -0.5)
        ones = const.tile([P, P], BF16, name="ones")
        nc.vector.memset(ones[:], 1.0)
        rows = const.tile([P, P], BF16, name="rows")
        nc.vector.memset(rows[:], 0.0)
        brow = const.tile([P, BLOCKS * J_OUT], BF16, name="brow")
        nc.vector.memset(brow[:], 0.0)
        nc.scalar.dma_start(out=rows[0:16, :], in_=g6.rearrange("b (c q) -> (b c) q", q=P))
        nc.scalar.dma_start(out=rows[16:32, :], in_=be6.rearrange("b (c q) -> (b c) q", q=P))
        nc.scalar.dma_start(out=brow[0:1, :], in_=b7.rearrange("(o b) j -> o (b j)", o=1))
        junk = const.tile([P, GROUP_ROWS], BF16, name="junk")
        gb = const.tile([P, 32], F32, name="gb")
        bias = const.tile([P, BLOCKS, J_OUT], F32, name="bias")
        wc = const.tile([P, BLOCKS, PASSES * J_OUT], U32, name="wc", align_bytes=64)
        ws = const.tile([P, BLOCKS, PASSES * J_OUT], U8, name="ws", align_bytes=64)

        def grouped_views(dst, src):
            return (dst.rearrange("p (c i) t -> p c t i", i=RUN),
                    src.rearrange("p t (c i) -> p c t i", i=RUN))

        nat_of = {}
        w_nat = {}
        queue = []
        for s in range(STEPS):
            if s == HALVES:
                queue.append(("w", 0))
            queue.append(("x", s))
        queue.append(("w", 1))
        issued = [0]

        def next_load():
            if issued[0] == len(queue):
                return
            kind, s = queue[issued[0]]
            issued[0] = issued[0] + 1
            if kind == "w":
                wn = natp.tile([P, 4, K_IN], BF16, name="nat")
                nc.sync.dma_start(out=wn[:], in_=W7[s].rearrange("(a o) k -> o a k", o=P))
                w_nat[s] = wn
                next_load()
                return
            b, h = divmod(s, HALVES)
            r, g = divmod(h, PASSES)
            nat = natp.tile([P, TILES, K_PASS], BF16, name="nat")
            nc.sync.dma_start(
                out=nat[:],
                in_=h6_pre[b, r * GROUP_ROWS:(r + 1) * GROUP_ROWS, g * K_PASS:(g + 1) * K_PASS]
                .rearrange("(q t) k -> q t k", t=TILES))
            nat_of[s] = nat

        for i in range(LOADS_AHEAD):
            next_load()

        warm_acc = accp.tile([P, J_OUT], F32, name="acc")
        for i in range(WARM_UP):
            nc.tensor.matmul(out=warm_acc[:, 0:P], lhsT=ones[:], rhs=ones[:], start=True, stop=True)

        def small_params():
            tp0 = tps.tile([P, TILES, P], BF16, name="tp")
            nc.tensor.transpose(tp0[:, 0, :], rows[:], ident[:])
            nc.vector.tensor_scalar(out=gb[:, 0:16], in0=tp0[:, 0, 0:16], scalar1=ROOT_ROWS, scalar2=None,
                                    op0=ALU.mult)
            nc.vector.tensor_copy(out=gb[:, 16:32], in_=tp0[:, 0, 16:32])
            for b in range(BLOCKS):
                acc = accp.tile([P, J_OUT], F32, name="acc")
                nc.tensor.matmul(out=acc[:], lhsT=ones[:], rhs=brow[:, b * J_OUT:(b + 1) * J_OUT],
                                 start=True, stop=True)
                nc.vector.tensor_copy(out=bias[:, b, :], in_=acc[:])

        st = {}
        xts = {}

        def open_block(b):
            sp = S_PATH[b]
            d = {}
            d["sq"] = statp.tile([P, PASSES * sp, GROUPS], F32, name="sq")
            if WIDE_SUMS[b]:
                d["part"] = statp.tile([P, PASSES * sp, GROUPS], F32, name="part")
            else:
                d["sums"] = sump.tile([P, 512], F32, name="sums")
            if sp < PACK:
                d["bst"] = statp.tile([P, PASSES * (PACK - sp), 2 * GROUPS, 6], F32, name="bst")
            st[b] = d

        def bank(s, x, vector_copies=False):
            b, h = divmod(s, HALVES)
            r, g = divmod(h, PASSES)
            sp = S_PATH[b]
            d = st[b]
            nat = nat_of[s]
            xt = xts[s]
            tp = tps.tile([P, TILES, P], BF16, name="tp")
            for t in range(TILES):
                nc.tensor.transpose(tp[:, t, :], nat[:, t, x * P:(x + 1) * P], ident[:])
            flat = tp[:].rearrange("q t n -> q (t n)")
            if x < sp:
                if WIDE_SUMS[b]:
                    n_sum = 512 // (PASSES * sp)
                    col = (g * sp + x) * n_sum
                    if col == 0:
                        d["sums"] = accp.tile([P, 512], F32, name="acc")
                else:
                    n_sum = 512 // (HALVES * sp)
                    col = (h * sp + x) * n_sum
                for t in range(TILES):
                    nc.tensor.matmul(out=d["sums"][:, col:col + n_sum], lhsT=nat[:, t, x * P:(x + 1) * P],
                                     rhs=ones[:, 0:n_sum], start=(t == 0), stop=(t == TILES - 1))
                if vector_copies:
                    nc.vector.tensor_copy(out=xt[:, x, :], in_=flat)
                    flat = xt[:, x, :]
                else:
                    nc.scalar.copy(out=xt[:, x, :].bitcast(F32), in_=flat.bitcast(F32))
                nc.scalar.activation(out=junk[:], in_=flat, func=ACT.Square, bias=xts[b * HALVES + g][:, x, 0:1],
                                     scale=-1.0, accum_out=d["sq"][:, g * sp + x, r:r + 1])
            else:
                nc.vector.tensor_copy(out=xt[:, x, :], in_=flat)
                for hh in range(2):
                    nc.vector.bn_stats(out=d["bst"][:, g * (PACK - sp) + x - sp, 2 * r + hh, :],
                                       in_=flat[:, hh * 512:(hh + 1) * 512])

        def w_transpose(b):
            wn = w_nat[b]
            wgr = grp.tile([P, PASSES, J_OUT, PACK], BF16, name="gr", align_bytes=64)
            for g in range(PASSES):
                for h in range(2):
                    tp = tps.tile([P, TILES, P], BF16, name="tp")
                    for t in range(PACK):
                        for a in range(2):
                            c = g * PACK + t
                            nc.tensor.transpose(tp[:, 2 * t + a, :], wn[:, 2 * h + a, c * P:(c + 1) * P], ident[:])
                    dst = wgr[:, g, 256 * h:256 * (h + 1), :].rearrange("p (a j) t -> p a j t", a=2)
                    src = tp[:].rearrange("p (t a) j -> p a j t", a=2)
                    if b == 0:
                        nc.vector.tensor_copy(out=dst, in_=src)
                    else:
                        nc.scalar.copy(out=dst, in_=src)
            return wgr

        def w_quantise(b, wgr):
            nc.vector.quantize_mx(out=wc[:, b, :].bitcast(FP8X4), scales=ws[:, b, :],
                                  in_=wgr[:].rearrange("p g n t -> p (g n t)"))

        def finish_stats(b):
            sp = S_PATH[b]
            d = st[b]
            w = PASSES * sp
            s1 = statp.tile([P, PASSES, sp], F32, name="s1")
            s2 = statp.tile([P, PASSES, sp], F32, name="s2")
            df = statp.tile([P, PASSES, sp], F32, name="df")
            mean = statp.tile([P, PASSES, PACK], F32, name="mean")
            varn = statp.tile([P, PASSES, PACK], F32, name="varn")
            rs = statp.tile([P, PASSES * PACK], F32, name="rs")
            sc = statp.tile([P, PASSES * PACK], F32, name="sc")
            bi = statp.tile([P, PASSES * PACK], F32, name="bi")
            if WIDE_SUMS[b]:
                nc.vector.tensor_reduce(out=s1[:].rearrange("q g x -> q (g x)"), in_=d["part"][:], axis=AX.X, op=ALU.add)
            else:
                nc.vector.tensor_reduce(
                    out=s1[:].rearrange("q g x -> q (g x)"),
                    in_=d["sums"][:].rearrange("q (r c n) -> q c r n", r=GROUPS, c=w)[:, :, :, 0],
                    axis=AX.X, op=ALU.add)
            nc.gpsimd.tensor_scalar(out=mean[:, :, 0:sp], in0=s1[:], scalar1=1.0 / ROWS, scalar2=0.0,
                                    op0=ALU.mult, op1=ALU.add)
            for g in range(PASSES):
                nc.gpsimd.tensor_tensor(out=df[:, g, :], in0=mean[:, g, 0:sp], in1=xts[b * HALVES + g][:, 0:sp, 0],
                                        op=ALU.subtract)
            nc.gpsimd.tensor_scalar(out=s1[:], in0=df[:], scalar1=float(ROWS), scalar2=0.0, op0=ALU.mult, op1=ALU.add)
            nc.gpsimd.tensor_tensor(out=df[:], in0=df[:], in1=s1[:], op=ALU.mult)
            if sp < PACK:
                mvv = statp.tile([P, PASSES, PACK - sp, 2], F32, name="mvv")
                for g in range(PASSES):
                    for x in range(PACK - sp):
                        nc.vector.bn_aggr(out=mvv[:, g, x, :],
                                          in_=d["bst"][:, g * (PACK - sp) + x, :, :].rearrange("q a s -> q (a s)"))
                nc.gpsimd.tensor_scalar(out=mean[:, :, sp:PACK], in0=mvv[:, :, :, 0], scalar1=1.0, scalar2=0.0,
                                        op0=ALU.mult, op1=ALU.add)
                nc.gpsimd.tensor_scalar(out=varn[:, :, sp:PACK], in0=mvv[:, :, :, 1], scalar1=float(ROWS), scalar2=0.0,
                                        op0=ALU.mult, op1=ALU.add)
            nc.vector.tensor_reduce(out=s2[:].rearrange("q g x -> q (g x)"), in_=d["sq"][:], axis=AX.X, op=ALU.add)
            nc.gpsimd.tensor_tensor(out=varn[:, :, 0:sp], in0=s2[:], in1=df[:], op=ALU.subtract)
            flat_var = varn[:].rearrange("q g x -> q (g x)")
            flat_mean = mean[:].rearrange("q g x -> q (g x)")
            nc.gpsimd.tensor_scalar(out=rs[:], in0=flat_var, scalar1=0.0, scalar2=EPS * ROWS, op0=ALU.max, op1=ALU.add)
            nc.gpsimd.tensor_tensor(out=rs[:], in0=rs[:], in1=mhalf[:], op=ALU.pow)
            nc.gpsimd.tensor_tensor(out=sc[:], in0=gb[:, b * 8:b * 8 + 8], in1=rs[:], op=ALU.mult)
            nc.gpsimd.tensor_tensor(out=rs[:], in0=flat_mean, in1=sc[:], op=ALU.mult)
            nc.gpsimd.tensor_tensor(out=bi[:], in0=gb[:, 16 + b * 8:16 + b * 8 + 8], in1=rs[:], op=ALU.subtract)
            d["sc"] = sc
            d["bi"] = bi

        work = {}

        def norms(s):
            b, h = divmod(s, HALVES)
            g = h % PASSES
            d = st[b]
            xt = xts[s]
            pl = plp.tile([P, PACK, GROUP_ROWS], BF16, name="pl")
            for x in range(PACK):
                c = g * PACK + x
                nc.vector.tensor_scalar(out=pl[:, x, :], in0=xt[:, x, :], scalar1=d["sc"][:, c:c + 1],
                                        scalar2=d["bi"][:, c:c + 1], op0=ALU.mult, op1=ALU.add)
            work[s] = {"pl": pl}

        def regroup(s):
            b = s // HALVES
            pl = work[s]["pl"]
            gr = grp.tile([P, GROUP_ROWS, PACK], BF16, name="gr", align_bytes=64)
            cv = GROUP_ROWS
            if b == 1:
                cv = 512 if s == HALVES else V_ROWS_BLOCK1
            if cv < GROUP_ROWS:
                da, sa = grouped_views(gr[:, cv:GROUP_ROWS, :], pl[:, :, cv:GROUP_ROWS])
                nc.scalar.activation(out=da, in_=sa, func=ACT.Relu)
            if cv > 0:
                dv, sv = grouped_views(gr[:, 0:cv, :], pl[:, :, 0:cv])
                nc.vector.tensor_scalar(out=dv, in0=sv, scalar1=0.0, scalar2=None, op0=ALU.max)
            work[s]["gr"] = gr

        def quantise(s):
            codes = acp.tile([P, GROUP_ROWS], U32, name="codes", align_bytes=64)
            scales = acp.tile([P, GROUP_ROWS], U8, name="scales", align_bytes=64)
            nc.vector.quantize_mx(out=codes[:].bitcast(FP8X4), scales=scales[:],
                                  in_=work[s]["gr"][:].rearrange("p n t -> p (n t)"))
            work[s]["codes"] = codes
            work[s]["scales"] = scales

        def multiply(m, hb):
            b = m // GROUPS
            accs = []
            for tt in range(4):
                t = 4 * hb + tt
                acc = accp.tile([P, J_OUT], F32, name="acc")
                for g in range(PASSES):
                    wk = work[PASSES * m + g]
                    nc.tensor.matmul_mx(out=acc[:], lhsT=wk["codes"][:, t * P:(t + 1) * P].bitcast(FP8X4),
                                        lhsT_scale=wk["scales"][:, t * P:(t + 1) * P],
                                        rhs=wc[:, b, g * J_OUT:(g + 1) * J_OUT].bitcast(FP8X4),
                                        rhs_scale=ws[:, b, g * J_OUT:(g + 1) * J_OUT],
                                        start=(g == 0), stop=(g == PASSES - 1))
                accs.append(acc)
            work[("acc", m, hb)] = accs

        def add_bias_and_store(m, hb):
            b, r = divmod(m, GROUPS)
            accs = work[("acc", m, hb)]
            osb = osbp.tile([P, 4, J_OUT], F32, name="osb")
            for tt in range(4):
                nc.vector.tensor_tensor(out=osb[:, tt, :], in0=accs[tt][:], in1=bias[:, b, :], op=ALU.add)
            dram = out[b, r * GROUP_ROWS:(r + 1) * GROUP_ROWS, :].rearrange("(q t) j -> q t j", t=TILES)
            nc.sync.dma_start(out=dram[:, 4 * hb:4 * hb + 4, :], in_=osb[:])

        open_block(0)
        wgrs = {}
        for s in range(HALVES):
            xts[s] = xtp.tile([P, PACK, GROUP_ROWS], BF16, name="xt")
            for x in BANK_ORDER:
                bank(s, x)
            if WIDE_SUMS[0] and s % PASSES == PASSES - 1:
                nc.vector.tensor_copy(out=st[0]["part"][:, :, s // PASSES],
                                      in_=st[0]["sums"][:].rearrange("q (c n) -> q c n", c=PASSES * S_PATH[0])[:, :, 0])
            next_load()
            if s == 3:
                small_params()
        finish_stats(0)
        wgrs[0] = w_transpose(0)
        open_block(1)

        def slot_of(s):
            return s + (BUBBLE if s >= HALVES else 0)

        quantise_at = {}
        norm_at = {}
        multiply_at = {}
        store_at = {}
        for q in range(-1, slot_of(STEPS - 1) + 3):
            norm_at[q] = []
        for s in range(STEPS):
            quantise_at[slot_of(s)] = s
            if s < HALVES:
                norm_at[slot_of(s) - 1].append(s)
            else:
                norm_at[max(slot_of(s) - 2, slot_of(HALVES) - 1)].append(s)
        for m in range(BLOCKS * GROUPS):
            for hb in range(2):
                multiply_at[slot_of(PASSES * m + 1) + hb] = (m, hb)
                store_at[slot_of(PASSES * m + 1) + hb + 1] = (m, hb)

        for s in range(HALVES, HALVES + PRE):
            xts[s] = xtp.tile([P, PACK, GROUP_ROWS], BF16, name="xt")
            for x in range(PACK):
                bank(s, x, True)
            next_load()
        norms(0)
        regroup(0)
        for q in range(slot_of(STEPS - 1) + 3):
            s1 = HALVES + PRE + q
            first = s1 < STEPS
            if first:
                xts[s1] = xtp.tile([P, PACK, GROUP_ROWS], BF16, name="xt")
                bank(s1, 0)
                bank(s1, 1)
            for s in norm_at[q]:
                norms(s)
            if q in quantise_at:
                quantise(quantise_at[q])
            if q == 0:
                w_quantise(0, wgrs[0])
            if q == slot_of(HALVES):
                w_quantise(1, wgrs[1])
            if q in store_at:
                add_bias_and_store(store_at[q][0], store_at[q][1])
            if first:
                bank(s1, 2)
                bank(s1, 3)
                next_load()
            if q in multiply_at:
                multiply(multiply_at[q][0], multiply_at[q][1])
            for s in norm_at[q]:
                regroup(s)
            if s1 == STEPS - 1:
                finish_stats(1)
                wgrs[1] = w_transpose(1)
